import numpy as np
import ml_dtypes


def mxq(x, axis, fmt="e4m3"):
    dtype, down = {"e4m3": (ml_dtypes.float8_e4m3fn, 7), "e5m2": (ml_dtypes.float8_e5m2, 14)}[fmt]
    v = np.moveaxis(np.asarray(x, np.float32).astype(ml_dtypes.bfloat16).astype(np.float64), axis, -1)
    blocks = v.reshape(v.shape[:-1] + (-1, 32))
    amax = np.abs(blocks).max(-1, keepdims=True)
    byte = np.maximum(np.where(amax > 0, np.frexp(amax)[1] - 1 + 127, 0) - down, 1)
    scale = np.exp2(byte - 127.0)
    codes = (blocks / scale).astype(np.float32).astype(dtype).astype(np.float64)
    return np.moveaxis((codes * scale).reshape(v.shape), -1, axis)


WIDE = False


def mx_kscale(k):
    if not WIDE:
        return np.ones(k)
    levels = np.array([10, -10, 5, -5, 0])
    a = np.random.permutation(np.resize(levels, k // 512 * 4)).reshape(k // 512, 4)
    idx = np.arange(k)
    return np.exp2(a[idx // 512, idx % 128 // 32])


BF16 = ml_dtypes.bfloat16


def bf(x):
    return np.asarray(x, np.float32).astype(BF16)


def f64(x):
    return np.asarray(x).astype(np.float64)


E2M1 = np.array([0.0, 0.5, 1.0, 1.5, 2.0, 3.0, 4.0, 6.0, -0.0, -0.5, -1.0, -1.5, -2.0, -3.0, -4.0, -6.0])


def pack_weight(w, fmt):
    k, n = w.shape
    w = f64(bf(w)).reshape(k // 32, 32, n)
    amax = np.abs(w).max(1)
    if fmt == "e4m3":
        byte = np.frexp(amax)[1] - 1 + 127 - 7
    else:
        mant, ex = np.frexp(amax / 6.0)
        byte = np.where(mant > 0.5, ex, ex - 1) + 127
    byte = np.clip(np.where(amax > 0, byte, 1), 1, 254)
    scaled = (w * np.exp2(127.0 - byte)[:, None, :]).reshape(k, n).astype(np.float32)
    by_word = np.ascontiguousarray(scaled.reshape(k // 512, 128, 4, n).transpose(0, 1, 3, 2))
    if fmt == "e4m3":
        words = by_word.astype(ml_dtypes.float8_e4m3fn).view(np.uint8)
    else:
        c = by_word.astype(ml_dtypes.float4_e2m1fn).view(np.uint8) & 0xF
        words = c[..., 0::2] | (c[..., 1::2] << 4)
    return np.ascontiguousarray(words), np.ascontiguousarray(byte.astype(np.uint8).reshape(k // 512, 16, n))


def unpack_weight(words, scales, fmt):
    g, p, n, _ = words.shape
    if fmt == "e4m3":
        vals = np.ascontiguousarray(words).view(ml_dtypes.float8_e4m3fn).astype(np.float64)
    else:
        nib = np.empty((g, p, n, 4), np.uint8)
        nib[..., 0::2] = words & 0xF
        nib[..., 1::2] = words >> 4
        vals = E2M1[nib]
    vals = vals * np.repeat(np.exp2(scales.astype(np.float64) - 127.0), 8, axis=1)[..., None]
    return vals.transpose(0, 1, 3, 2).reshape(g * 512, n)


B, C, H, W, HS, WS = 4, 1024, 16, 16, 16, 32
N = H * W
EPS = 1e-5


def mean_variance_norm(flat):
    mu = flat.mean(axis=-1, keepdims=True)
    sd = np.sqrt(flat.var(axis=-1, ddof=1, keepdims=True) + EPS)
    return (flat - mu) / sd


def setup_inputs():
    s = mx_kscale(C)
    gain = 0.7 + 0.6 * np.random.random_sample((B, C, 1, 1))
    shift = 0.4 * np.random.standard_normal((B, C, 1, 1))
    content = bf(np.random.standard_normal((B, C, H, W)) * gain + shift)
    mean = bf(np.random.standard_normal((B, C, H, W)) * 0.3 * s[:, None, None])
    std = bf(np.abs(1.0 + 0.25 * np.random.standard_normal((B, C, H, W))) * s[:, None, None])
    out_w = np.random.standard_normal((C, C)) / np.sqrt(C) / s
    words, scales = pack_weight(out_w.T, "e4m3")
    out_b = bf(np.random.standard_normal(C) * 0.2)
    return {"content": content,
            "mean": mean,
            "std": std,
            "out_w_words": words,
            "out_w_scales": scales,
            "out_b": out_b}


def reference(content, mean, std, out_w_words, out_w_scales, out_b):
    x = f64(content).reshape(B, C, N)
    o = f64(std).reshape(B, C, N) * mean_variance_norm(x) + f64(mean).reshape(B, C, N)
    y = (unpack_weight(out_w_words, out_w_scales, "e4m3").T @ mxq(o, 1, "e4m3")) + f64(out_b)[:, None]
    return (y + x).reshape(B, C, H, W)

@@ -1,0 +1,236 @@
+from contextlib import ExitStack
+
+import concourse.mybir as mybir
+from concourse.masks import make_identity
+
+F32 = mybir.dt.float32
+BF16 = mybir.dt.bfloat16
+I32 = mybir.dt.int32
+U32 = mybir.dt.uint32
+U8 = mybir.dt.uint8
+FP8X4 = mybir.dt.float8_e4m3fn_x4
+ACT = mybir.ActivationFunctionType
+ALU = mybir.AluOpType
+
+IMAGES = 4
+CHANNELS = 1024
+PIXELS = 256
+EPS = 1e-5
+
+P = 128
+PACK = 4
+K_PASS = P * PACK
+PASSES = CHANNELS // K_PASS
+CHUNKS = IMAGES * PASSES
+CO_TILES = CHANNELS // P
+TILES_PER_BANK = 2
+BANKS_PER_IMAGE = CO_TILES // TILES_PER_BANK
+RUN = 4
+
+FLOPS = 2 * IMAGES * PIXELS * CHANNELS * CHANNELS
+
+
+def tile_aattn_pb_kernel(tc, content, mean, std, out_w_words, out_w_scales, out_b, out):
+    nc = tc.nc
+
+    by_k = "b (g p t) h w -> b g p t (h w)"
+    by_co = "b (j m) h w -> b m j (h w)"
+    content_k = content.rearrange(by_k, g=PASSES, p=P, t=PACK)
+    std_k = std.rearrange(by_k, g=PASSES, p=P, t=PACK)
+    mean_k = mean.rearrange(by_k, g=PASSES, p=P, t=PACK)
+    content_co = content.rearrange(by_co, m=P)
+    out_co = out.rearrange(by_co, m=P)
+
+    with ExitStack() as ctx:
+        consts = ctx.enter_context(tc.tile_pool(name="consts", bufs=1))
+        inputs = ctx.enter_context(tc.tile_pool(name="inputs", bufs=CHUNKS))
+        residuals = ctx.enter_context(tc.tile_pool(name="residuals", bufs=IMAGES))
+        stats_pool = ctx.enter_context(tc.tile_pool(name="stats", bufs=4))
+        unread = ctx.enter_context(tc.tile_pool(name="unread", bufs=8))
+        work = ctx.enter_context(tc.tile_pool(name="work", bufs=3))
+        quantised = ctx.enter_context(tc.tile_pool(name="quantised", bufs=2))
+        results = ctx.enter_context(tc.tile_pool(name="results", bufs=6))
+
+        eps = consts.tile([P, 1], F32)
+        nc.vector.memset(eps[:], EPS)
+        table_warm = consts.tile([P, 1], F32)
+        nc.scalar.activation(out=table_warm[:], in_=eps[:], func=ACT.Sqrt)
+
+        w_words = consts.tile([P, PASSES, CHANNELS], U32, align_bytes=64)
+        w_scales = consts.tile([P, PASSES, CHANNELS], U8, align_bytes=64)
+        nc.vector.memset(w_scales[:].rearrange("p g n -> p (g n)").bitcast(I32), 0)
+
+        identity = consts.tile([P, P], BF16)
+        make_identity(nc, identity[:])
+        bias_rows = consts.tile([P, P], BF16)
+        nc.gpsimd.memset(bias_rows[:], 0.0)
+
+        x_k, std_in, mean_in, x_co = [], [], [], []
+
+        def load_content(b):
+            for g in range(PASSES):
+                x = inputs.tile([P, PACK, PIXELS], BF16, tag="x")
+                nc.sync.dma_start(out=x[:], in_=content_k[b, g])
+                x_k.append(x)
+
+        def load_modulation(b):
+            for g in range(PASSES):
+                s = inputs.tile([P, PACK, PIXELS], BF16, tag="s")
+                nc.sync.dma_start(out=s[:], in_=std_k[b, g])
+                std_in.append(s)
+                m = inputs.tile([P, PACK, PIXELS], BF16, tag="m")
+                nc.sync.dma_start(out=m[:], in_=mean_k[b, g])
+                mean_in.append(m)
+
+        def load_weight():
+            for quadrant in range(4):
+                rows = slice(4 * quadrant, 4 * quadrant + 4)
+                nc.sync.dma_start(
+                    out=w_scales[32 * quadrant : 32 * quadrant + 4, :, :].bitcast(I32),
+                    in_=out_w_scales[:, rows, :].rearrange("g r n -> r g n").bitcast(I32),
+                )
+            for g in range(PASSES):
+                nc.sync.dma_start(
+                    out=w_words[:, g, :].bitcast(I32),
+                    in_=out_w_words[g].rearrange("p n t -> p (n t)").bitcast(I32),
+                )
+            nc.sync.dma_start(out=bias_rows[0:CO_TILES, :], in_=out_b.rearrange("(j m) -> j m", m=P))
+
+        def load_residual(b):
+            r = residuals.tile([P, CO_TILES, PIXELS], BF16, tag="r")
+            nc.sync.dma_start(out=r[:], in_=content_co[b])
+            x_co.append(r)
+
+        for b in range(IMAGES):
+            load_content(b)
+            if b == 1:
+                load_weight()
+            load_modulation(b)
+            if b >= 1:
+                load_residual(b - 1)
+        load_residual(IMAGES - 1)
+
+        bias = consts.tile([P, CO_TILES], F32)
+        with tc.psum_pool(name="setup_psum", bufs=1) as setup_psum:
+            bias_cols = setup_psum.tile([P, P], BF16)
+            nc.tensor.transpose(out=bias_cols[:], in_=bias_rows[:], identity=identity[:])
+            nc.vector.tensor_copy(out=bias[:], in_=bias_cols[:, 0:CO_TILES])
+
+        banks = ctx.enter_context(tc.psum_pool(name="banks", bufs=2 * BANKS_PER_IMAGE))
+
+        neg_mu, sd, o_rows, o_grouped, o_words, o_scales, acc = {}, {}, {}, {}, {}, {}, {}
+
+        def statistics(c):
+            total = stats_pool.tile([P, PACK], F32, tag="total")
+            for t in range(PACK):
+                copy_out = unread.tile([P, PIXELS], BF16, tag="unread")
+                nc.scalar.activation(
+                    out=copy_out[:], in_=x_k[c][:, t, :], func=ACT.Identity, accum_out=total[:, t : t + 1]
+                )
+            neg_mu[c] = stats_pool.tile([P, PACK], F32, name="neg_mu", tag="neg_mu")
+            nc.scalar.mul(out=neg_mu[c][:], in_=total[:], mul=-1.0 / PIXELS)
+            squares = stats_pool.tile([P, PACK], F32, tag="squares")
+            for t in range(PACK):
+                square_out = unread.tile([P, PIXELS], BF16, tag="unread")
+                nc.scalar.activation(
+                    out=square_out[:],
+                    in_=x_k[c][:, t, :],
+                    func=ACT.Square,
+                    bias=neg_mu[c][:, t : t + 1],
+                    accum_out=squares[:, t : t + 1],
+                )
+            sd[c] = stats_pool.tile([P, PACK], F32, name="sd", tag="sd")
+            nc.scalar.activation(
+                out=sd[c][:], in_=squares[:], func=ACT.Sqrt, bias=eps[:], scale=1.0 / (PIXELS - 1)
+            )
+
+        def modulate(c):
+            rstd = stats_pool.tile([P, PACK], F32, tag="rstd")
+            nc.vector.reciprocal(out=rstd[:], in_=sd[c][:])
+            centred = work.tile([P, PACK, PIXELS], F32, tag="centred")
+            o_rows[c] = work.tile([P, PACK, PIXELS], BF16, name="o_rows", tag="o_rows")
+            for t in range(PACK):
+                nc.vector.scalar_tensor_tensor(
+                    out=centred[:, t, :],
+                    in0=x_k[c][:, t, :],
+                    scalar=neg_mu[c][:, t : t + 1],
+                    in1=std_in[c][:, t, :],
+                    op0=ALU.add,
+                    op1=ALU.mult,
+                )
+            for t in range(PACK):
+                nc.vector.scalar_tensor_tensor(
+                    out=o_rows[c][:, t, :],
+                    in0=centred[:, t, :],
+                    scalar=rstd[:, t : t + 1],
+                    in1=mean_in[c][:, t, :],
+                    op0=ALU.mult,
+                    op1=ALU.add,
+                )
+
+        def regroup(c):
+            o_grouped[c] = work.tile([P, PIXELS, PACK], BF16, name="o_grouped", tag="o_grouped", align_bytes=64)
+            nc.scalar.copy(
+                out=o_grouped[c][:].rearrange("p (n i) t -> p n t i", i=RUN),
+                in_=o_rows[c][:].rearrange("p t (n i) -> p n t i", i=RUN),
+            )
+
+        def quantise(c):
+            b, g = divmod(c, PASSES)
+            if g == 0:
+                o_words[b] = quantised.tile([P, PASSES, PIXELS], U32, name="o_words", tag="o_words", align_bytes=64)
+                o_scales[b] = quantised.tile([P, PASSES, PIXELS], U8, name="o_scales", tag="o_scales", align_bytes=64)
+            nc.vector.quantize_mx(
+                out=o_words[b][:, g, :].bitcast(FP8X4),
+                scales=o_scales[b][:, g, :],
+                in_=o_grouped[c][:].rearrange("p n t -> p (n t)"),
+            )
+
+        def project(b):
+            acc[b] = []
+            for bank in range(BANKS_PER_IMAGE):
+                pair = banks.tile([P, TILES_PER_BANK, PIXELS], F32, tag="pair")
+                for half in range(TILES_PER_BANK):
+                    j = bank * TILES_PER_BANK + half
+                    cols = slice(j * P, (j + 1) * P)
+                    for g in range(PASSES):
+                        nc.tensor.matmul_mx(
+                            out=pair[:, half, :],
+                            lhsT=w_words[:, g, cols].bitcast(FP8X4),
+                            lhsT_scale=w_scales[:, g, cols],
+                            rhs=o_words[b][:, g, :].bitcast(FP8X4),
+                            rhs_scale=o_scales[b][:, g, :],
+                            start=(g == 0),
+                            stop=(g == PASSES - 1),
+                        )
+                acc[b].append(pair)
+
+        def finish(b):
+            for bank in range(BANKS_PER_IMAGE):
+                y = results.tile([P, TILES_PER_BANK, PIXELS], F32, tag="y")
+                first = bank * TILES_PER_BANK
+                for half in range(TILES_PER_BANK):
+                    j = first + half
+                    nc.vector.scalar_tensor_tensor(
+                        out=y[:, half, :],
+                        in0=acc[b][bank][:, half, :],
+                        scalar=bias[:, j : j + 1],
+                        in1=x_co[b][:, j, :],
+                        op0=ALU.add,
+                        op1=ALU.add,
+                    )
+                nc.sync.dma_start(out=out_co[b, :, first : first + TILES_PER_BANK, :], in_=y[:])
+
+        for s in range(CHUNKS + 3):
+            if 0 <= s - 2 < CHUNKS:
+                regroup(s - 2)
+            if s < CHUNKS:
+                statistics(s)
+            if 0 <= s - 1 < CHUNKS:
+                modulate(s - 1)
+            if s - 3 >= 0 and (s - 3) % PASSES == PASSES - 1 and (s - 3) // PASSES < IMAGES:
+                finish((s - 3) // PASSES)
+            if 0 <= s - 2 < CHUNKS:
+                quantise(s - 2)
+                if (s - 2) % PASSES == PASSES - 1:
+                    project((s - 2) // PASSES)

@@ -23,8 +23,7 @@ K_PASS = P * PACK
 PASSES = CHANNELS // K_PASS
 CHUNKS = IMAGES * PASSES
 CO_TILES = CHANNELS // P
-TILES_PER_BANK = 2
-BANKS_PER_IMAGE = CO_TILES // TILES_PER_BANK
+TILES_PER_STORE = 2
 RUN = 4
 
 FLOPS = 2 * IMAGES * PIXELS * CHANNELS * CHANNELS
@@ -116,7 +115,7 @@ def tile_aattn_pb_kernel(tc, content, mean, std, out_w_words, out_w_scales, out_
             nc.tensor.transpose(out=bias_cols[:], in_=bias_rows[:], identity=identity[:])
             nc.vector.tensor_copy(out=bias[:], in_=bias_cols[:, 0:CO_TILES])
 
-        banks = ctx.enter_context(tc.psum_pool(name="banks", bufs=2 * BANKS_PER_IMAGE))
+        banks = ctx.enter_context(tc.psum_pool(name="banks", bufs=CO_TILES))
 
         neg_mu, sd, o_rows, o_grouped, o_words, o_scales, acc = {}, {}, {}, {}, {}, {}, {}
 
@@ -142,6 +141,20 @@ def tile_aattn_pb_kernel(tc, content, mean, std, out_w_words, out_w_scales, out_
             sd[c] = stats_pool.tile([P, PACK], F32, name="sd", tag="sd")
             nc.scalar.activation(
                 out=sd[c][:], in_=squares[:], func=ACT.Sqrt, bias=eps[:], scale=1.0 / (PIXELS - 1)
+            )
+
+        def statistics_on_vector(c):
+            moments = stats_pool.tile([P, PACK, 6], F32, tag="moments")
+            mean_var = stats_pool.tile([P, PACK, 2], F32, tag="mean_var")
+            for t in range(PACK):
+                nc.vector.bn_stats(out=moments[:, t, :], in_=x_k[c][:, t, :])
+            for t in range(PACK):
+                nc.vector.bn_aggr(out=mean_var[:, t, :], in_=moments[:, t, :])
+            neg_mu[c] = stats_pool.tile([P, PACK], F32, name="neg_mu", tag="neg_mu")
+            nc.vector.tensor_scalar_mul(out=neg_mu[c][:], in0=mean_var[:, :, 0], scalar1=-1.0)
+            sd[c] = stats_pool.tile([P, PACK], F32, name="sd", tag="sd")
+            nc.scalar.activation(
+                out=sd[c][:], in_=mean_var[:, :, 1], func=ACT.Sqrt, bias=eps[:], scale=PIXELS / (PIXELS - 1.0)
             )
 
         def modulate(c):
@@ -186,51 +199,51 @@ def tile_aattn_pb_kernel(tc, content, mean, std, out_w_words, out_w_scales, out_
                 in_=o_grouped[c][:].rearrange("p n t -> p (n t)"),
             )
 
-        def project(b):
-            acc[b] = []
-            for bank in range(BANKS_PER_IMAGE):
-                pair = banks.tile([P, TILES_PER_BANK, PIXELS], F32, tag="pair")
-                for half in range(TILES_PER_BANK):
-                    j = bank * TILES_PER_BANK + half
-                    cols = slice(j * P, (j + 1) * P)
-                    for g in range(PASSES):
-                        nc.tensor.matmul_mx(
-                            out=pair[:, half, :],
-                            lhsT=w_words[:, g, cols].bitcast(FP8X4),
-                            lhsT_scale=w_scales[:, g, cols],
-                            rhs=o_words[b][:, g, :].bitcast(FP8X4),
-                            rhs_scale=o_scales[b][:, g, :],
-                            start=(g == 0),
-                            stop=(g == PASSES - 1),
-                        )
-                acc[b].append(pair)
+        def project(c):
+            b, g = divmod(c, PASSES)
+            if g == 0:
+                acc[b] = []
+                for j in range(CO_TILES):
+                    bank = banks.tile([P, PIXELS], F32, tag="bank")
+                    acc[b].append(bank)
+            for j in range(CO_TILES):
+                cols = slice(j * P, (j + 1) * P)
+                nc.tensor.matmul_mx(
+                    out=acc[b][j][:],
+                    lhsT=w_words[:, g, cols].bitcast(FP8X4),
+                    lhsT_scale=w_scales[:, g, cols],
+                    rhs=o_words[b][:, g, :].bitcast(FP8X4),
+                    rhs_scale=o_scales[b][:, g, :],
+                    start=(g == 0),
+                    stop=(g == PASSES - 1),
+                )
 
         def finish(b):
-            for bank in range(BANKS_PER_IMAGE):
-                y = results.tile([P, TILES_PER_BANK, PIXELS], F32, tag="y")
-                first = bank * TILES_PER_BANK
-                for half in range(TILES_PER_BANK):
-                    j = first + half
+            for first in range(0, CO_TILES, TILES_PER_STORE):
+                y = results.tile([P, TILES_PER_STORE, PIXELS], F32, tag="y")
+                for i in range(TILES_PER_STORE):
+                    j = first + i
                     nc.vector.scalar_tensor_tensor(
-                        out=y[:, half, :],
-                        in0=acc[b][bank][:, half, :],
+                        out=y[:, i, :],
+                        in0=acc[b][j][:],
                         scalar=bias[:, j : j + 1],
                         in1=x_co[b][:, j, :],
                         op0=ALU.add,
                         op1=ALU.add,
                     )
-                nc.sync.dma_start(out=out_co[b, :, first : first + TILES_PER_BANK, :], in_=y[:])
+                nc.sync.dma_start(out=out_co[b, :, first : first + TILES_PER_STORE, :], in_=y[:])
 
         for s in range(CHUNKS + 3):
             if 0 <= s - 2 < CHUNKS:
                 regroup(s - 2)
-            if s < CHUNKS:
+            if s == 0:
+                statistics_on_vector(s)
+            elif s < CHUNKS:
                 statistics(s)
             if 0 <= s - 1 < CHUNKS:
                 modulate(s - 1)
-            if s - 3 >= 0 and (s - 3) % PASSES == PASSES - 1 and (s - 3) // PASSES < IMAGES:
+            if s - 3 >= 0 and (s - 3) % PASSES == PASSES - 1:
                 finish((s - 3) // PASSES)
             if 0 <= s - 2 < CHUNKS:
                 quantise(s - 2)
-                if (s - 2) % PASSES == PASSES - 1:
-                    project((s - 2) // PASSES)
+                project(s - 2)

@@ -23,6 +23,7 @@ K_PASS = P * PACK
 PASSES = CHANNELS // K_PASS
 CHUNKS = IMAGES * PASSES
 CO_TILES = CHANNELS // P
+HALF = CO_TILES // 2
 TILES_PER_STORE = 2
 RUN = 4
 
@@ -32,7 +33,7 @@ FLOPS = 2 * IMAGES * PIXELS * CHANNELS * CHANNELS
 def tile_aattn_pb_kernel(tc, content, mean, std, out_w_words, out_w_scales, out_b, out):
     nc = tc.nc
 
-    by_k = "b (g p t) h w -> b g p t (h w)"
+    by_k = "b (g p t) h w -> (b g) p t (h w)"
     by_co = "b (j m) h w -> b m j (h w)"
     content_k = content.rearrange(by_k, g=PASSES, p=P, t=PACK)
     std_k = std.rearrange(by_k, g=PASSES, p=P, t=PACK)
@@ -44,7 +45,7 @@ def tile_aattn_pb_kernel(tc, content, mean, std, out_w_words, out_w_scales, out_
         consts = ctx.enter_context(tc.tile_pool(name="consts", bufs=1))
         inputs = ctx.enter_context(tc.tile_pool(name="inputs", bufs=CHUNKS))
         residuals = ctx.enter_context(tc.tile_pool(name="residuals", bufs=IMAGES))
-        stats_pool = ctx.enter_context(tc.tile_pool(name="stats", bufs=4))
+        stats = ctx.enter_context(tc.tile_pool(name="stats", bufs=4))
         unread = ctx.enter_context(tc.tile_pool(name="unread", bufs=8))
         work = ctx.enter_context(tc.tile_pool(name="work", bufs=3))
         quantised = ctx.enter_context(tc.tile_pool(name="quantised", bufs=2))
@@ -55,31 +56,28 @@ def tile_aattn_pb_kernel(tc, content, mean, std, out_w_words, out_w_scales, out_
         table_warm = consts.tile([P, 1], F32)
         nc.scalar.activation(out=table_warm[:], in_=eps[:], func=ACT.Sqrt)
 
+        bias_rows = consts.tile([P, P], BF16)
+        nc.vector.memset(bias_rows[:].bitcast(I32), 0)
         w_words = consts.tile([P, PASSES, CHANNELS], U32, align_bytes=64)
         w_scales = consts.tile([P, PASSES, CHANNELS], U8, align_bytes=64)
         nc.vector.memset(w_scales[:].rearrange("p g n -> p (g n)").bitcast(I32), 0)
-
         identity = consts.tile([P, P], BF16)
         make_identity(nc, identity[:])
-        bias_rows = consts.tile([P, P], BF16)
-        nc.gpsimd.memset(bias_rows[:], 0.0)
 
         x_k, std_in, mean_in, x_co = [], [], [], []
 
-        def load_content(b):
-            for g in range(PASSES):
-                x = inputs.tile([P, PACK, PIXELS], BF16, tag="x")
-                nc.sync.dma_start(out=x[:], in_=content_k[b, g])
-                x_k.append(x)
+        def load_content(c):
+            x = inputs.tile([P, PACK, PIXELS], BF16, tag="x")
+            nc.sync.dma_start(out=x[:], in_=content_k[c])
+            x_k.append(x)
 
-        def load_modulation(b):
-            for g in range(PASSES):
-                s = inputs.tile([P, PACK, PIXELS], BF16, tag="s")
-                nc.sync.dma_start(out=s[:], in_=std_k[b, g])
-                std_in.append(s)
-                m = inputs.tile([P, PACK, PIXELS], BF16, tag="m")
-                nc.sync.dma_start(out=m[:], in_=mean_k[b, g])
-                mean_in.append(m)
+        def load_modulation(c):
+            s = inputs.tile([P, PACK, PIXELS], BF16, tag="s")
+            nc.sync.dma_start(out=s[:], in_=std_k[c])
+            std_in.append(s)
+            m = inputs.tile([P, PACK, PIXELS], BF16, tag="m")
+            nc.sync.dma_start(out=m[:], in_=mean_k[c])
+            mean_in.append(m)
 
         def load_weight():
             for quadrant in range(4):
@@ -93,20 +91,23 @@ def tile_aattn_pb_kernel(tc, content, mean, std, out_w_words, out_w_scales, out_
                     out=w_words[:, g, :].bitcast(I32),
                     in_=out_w_words[g].rearrange("p n t -> p (n t)").bitcast(I32),
                 )
-            nc.sync.dma_start(out=bias_rows[0:CO_TILES, :], in_=out_b.rearrange("(j m) -> j m", m=P))
 
         def load_residual(b):
             r = residuals.tile([P, CO_TILES, PIXELS], BF16, tag="r")
             nc.sync.dma_start(out=r[:], in_=content_co[b])
             x_co.append(r)
 
-        for b in range(IMAGES):
-            load_content(b)
-            if b == 1:
+        for c in range(CHUNKS):
+            if c % PASSES == 0:
+                for g in range(PASSES):
+                    load_content(c + g)
+            if c == 0:
+                nc.sync.dma_start(out=bias_rows[0:CO_TILES, :], in_=out_b.rearrange("(j m) -> j m", m=P))
+            load_modulation(c)
+            if c == PASSES:
                 load_weight()
-            load_modulation(b)
-            if b >= 1:
-                load_residual(b - 1)
+            if c > PASSES and c % PASSES == PASSES - 1:
+                load_residual(c // PASSES - 1)
         load_residual(IMAGES - 1)
 
         bias = consts.tile([P, CO_TILES], F32)
@@ -117,18 +118,23 @@ def tile_aattn_pb_kernel(tc, content, mean, std, out_w_words, out_w_scales, out_
 
         banks = ctx.enter_context(tc.psum_pool(name="banks", bufs=CO_TILES))
 
-        neg_mu, sd, o_rows, o_grouped, o_words, o_scales, acc = {}, {}, {}, {}, {}, {}, {}
+        total, neg_mu, squares, sd, rstd = {}, {}, {}, {}, {}
+        centred, o_rows, o_grouped, o_words, o_scales, acc = {}, {}, {}, {}, {}, {}
 
-        def statistics(c):
-            total = stats_pool.tile([P, PACK], F32, tag="total")
+        def sum_pixels(c):
+            total[c] = stats.tile([P, PACK], F32, name="total", tag="total")
             for t in range(PACK):
                 copy_out = unread.tile([P, PIXELS], BF16, tag="unread")
                 nc.scalar.activation(
-                    out=copy_out[:], in_=x_k[c][:, t, :], func=ACT.Identity, accum_out=total[:, t : t + 1]
+                    out=copy_out[:], in_=x_k[c][:, t, :], func=ACT.Identity, accum_out=total[c][:, t : t + 1]
                 )
-            neg_mu[c] = stats_pool.tile([P, PACK], F32, name="neg_mu", tag="neg_mu")
-            nc.scalar.mul(out=neg_mu[c][:], in_=total[:], mul=-1.0 / PIXELS)
-            squares = stats_pool.tile([P, PACK], F32, tag="squares")
+
+        def negate_mean(c):
+            neg_mu[c] = stats.tile([P, PACK], F32, name="neg_mu", tag="neg_mu")
+            nc.scalar.mul(out=neg_mu[c][:], in_=total[c][:], mul=-1.0 / PIXELS)
+
+        def sum_squares(c):
+            squares[c] = stats.tile([P, PACK], F32, name="squares", tag="squares")
             for t in range(PACK):
                 square_out = unread.tile([P, PIXELS], BF16, tag="unread")
                 nc.scalar.activation(
@@ -136,46 +142,38 @@ def tile_aattn_pb_kernel(tc, content, mean, std, out_w_words, out_w_scales, out_
                     in_=x_k[c][:, t, :],
                     func=ACT.Square,
                     bias=neg_mu[c][:, t : t + 1],
-                    accum_out=squares[:, t : t + 1],
+                    accum_out=squares[c][:, t : t + 1],
                 )
-            sd[c] = stats_pool.tile([P, PACK], F32, name="sd", tag="sd")
+
+        def deviation(c):
+            sd[c] = stats.tile([P, PACK], F32, name="sd", tag="sd")
             nc.scalar.activation(
-                out=sd[c][:], in_=squares[:], func=ACT.Sqrt, bias=eps[:], scale=1.0 / (PIXELS - 1)
+                out=sd[c][:], in_=squares[c][:], func=ACT.Sqrt, bias=eps[:], scale=1.0 / (PIXELS - 1)
             )
 
-        def statistics_on_vector(c):
-            moments = stats_pool.tile([P, PACK, 6], F32, tag="moments")
-            mean_var = stats_pool.tile([P, PACK, 2], F32, tag="mean_var")
-            for t in range(PACK):
-                nc.vector.bn_stats(out=moments[:, t, :], in_=x_k[c][:, t, :])
-            for t in range(PACK):
-                nc.vector.bn_aggr(out=mean_var[:, t, :], in_=moments[:, t, :])
-            neg_mu[c] = stats_pool.tile([P, PACK], F32, name="neg_mu", tag="neg_mu")
-            nc.vector.tensor_scalar_mul(out=neg_mu[c][:], in0=mean_var[:, :, 0], scalar1=-1.0)
-            sd[c] = stats_pool.tile([P, PACK], F32, name="sd", tag="sd")
-            nc.scalar.activation(
-                out=sd[c][:], in_=mean_var[:, :, 1], func=ACT.Sqrt, bias=eps[:], scale=PIXELS / (PIXELS - 1.0)
-            )
-
-        def modulate(c):
-            rstd = stats_pool.tile([P, PACK], F32, tag="rstd")
-            nc.vector.reciprocal(out=rstd[:], in_=sd[c][:])
-            centred = work.tile([P, PACK, PIXELS], F32, tag="centred")
-            o_rows[c] = work.tile([P, PACK, PIXELS], BF16, name="o_rows", tag="o_rows")
+        def centre(c):
+            centred[c] = work.tile([P, PACK, PIXELS], F32, name="centred", tag="centred")
             for t in range(PACK):
                 nc.vector.scalar_tensor_tensor(
-                    out=centred[:, t, :],
+                    out=centred[c][:, t, :],
                     in0=x_k[c][:, t, :],
                     scalar=neg_mu[c][:, t : t + 1],
                     in1=std_in[c][:, t, :],
                     op0=ALU.add,
                     op1=ALU.mult,
                 )
+
+        def invert(c):
+            rstd[c] = stats.tile([P, PACK], F32, name="rstd", tag="rstd")
+            nc.vector.reciprocal(out=rstd[c][:], in_=sd[c][:])
+
+        def modulate(c):
+            o_rows[c] = work.tile([P, PACK, PIXELS], BF16, name="o_rows", tag="o_rows")
             for t in range(PACK):
                 nc.vector.scalar_tensor_tensor(
                     out=o_rows[c][:, t, :],
-                    in0=centred[:, t, :],
-                    scalar=rstd[:, t : t + 1],
+                    in0=centred[c][:, t, :],
+                    scalar=rstd[c][:, t : t + 1],
                     in1=mean_in[c][:, t, :],
                     op0=ALU.mult,
                     op1=ALU.add,
@@ -201,15 +199,12 @@ def tile_aattn_pb_kernel(tc, content, mean, std, out_w_words, out_w_scales, out_
 
         def project(c):
             b, g = divmod(c, PASSES)
-            if g == 0:
-                acc[b] = []
-                for j in range(CO_TILES):
-                    bank = banks.tile([P, PIXELS], F32, tag="bank")
-                    acc[b].append(bank)
             for j in range(CO_TILES):
+                if g == 0:
+                    acc[b, j] = banks.tile([P, PIXELS], F32, name="bank", tag="bank")
                 cols = slice(j * P, (j + 1) * P)
                 nc.tensor.matmul_mx(
-                    out=acc[b][j][:],
+                    out=acc[b, j][:],
                     lhsT=w_words[:, g, cols].bitcast(FP8X4),
                     lhsT_scale=w_scales[:, g, cols],
                     rhs=o_words[b][:, g, :].bitcast(FP8X4),
@@ -218,14 +213,14 @@ def tile_aattn_pb_kernel(tc, content, mean, std, out_w_words, out_w_scales, out_
                     stop=(g == PASSES - 1),
                 )
 
-        def finish(b):
-            for first in range(0, CO_TILES, TILES_PER_STORE):
+        def finish(b, half):
+            for first in range(half * HALF, (half + 1) * HALF, TILES_PER_STORE):
                 y = results.tile([P, TILES_PER_STORE, PIXELS], F32, tag="y")
                 for i in range(TILES_PER_STORE):
                     j = first + i
                     nc.vector.scalar_tensor_tensor(
                         out=y[:, i, :],
-                        in0=acc[b][j][:],
+                        in0=acc[b, j][:],
                         scalar=bias[:, j : j + 1],
                         in1=x_co[b][:, j, :],
                         op0=ALU.add,
@@ -233,17 +228,21 @@ def tile_aattn_pb_kernel(tc, content, mean, std, out_w_words, out_w_scales, out_
                     )
                 nc.sync.dma_start(out=out_co[b, :, first : first + TILES_PER_STORE, :], in_=y[:])
 
-        for s in range(CHUNKS + 3):
-            if 0 <= s - 2 < CHUNKS:
-                regroup(s - 2)
-            if s == 0:
-                statistics_on_vector(s)
-            elif s < CHUNKS:
-                statistics(s)
-            if 0 <= s - 1 < CHUNKS:
-                modulate(s - 1)
-            if s - 3 >= 0 and (s - 3) % PASSES == PASSES - 1:
-                finish((s - 3) // PASSES)
-            if 0 <= s - 2 < CHUNKS:
-                quantise(s - 2)
-                project(s - 2)
+        def on_chunk(stage, c):
+            if 0 <= c < CHUNKS:
+                stage(c)
+
+        with tc.manual_schedule():
+            for s in range(-1, CHUNKS + 3):
+                on_chunk(centre, s)
+                on_chunk(invert, s - 1)
+                on_chunk(quantise, s - 2)
+                on_chunk(project, s - 2)
+                on_chunk(modulate, s - 1)
+                if 0 <= s - 3 < CHUNKS:
+                    finish((s - 3) // PASSES, (s - 3) % PASSES)
+                on_chunk(sum_pixels, s + 1)
+                on_chunk(sum_squares, s)
+                on_chunk(negate_mean, s + 1)
+                on_chunk(regroup, s - 1)
+                on_chunk(deviation, s)

@@ -25,6 +25,7 @@ CHUNKS = IMAGES * PASSES
 CO_TILES = CHANNELS // P
 HALF = CO_TILES // 2
 TILES_PER_STORE = 2
+FINISH_LAG = 3
 RUN = 4
 
 FLOPS = 2 * IMAGES * PIXELS * CHANNELS * CHANNELS
@@ -49,7 +50,7 @@ def tile_aattn_pb_kernel(tc, content, mean, std, out_w_words, out_w_scales, out_
         unread = ctx.enter_context(tc.tile_pool(name="unread", bufs=8))
         work = ctx.enter_context(tc.tile_pool(name="work", bufs=3))
         quantised = ctx.enter_context(tc.tile_pool(name="quantised", bufs=2))
-        results = ctx.enter_context(tc.tile_pool(name="results", bufs=6))
+        results = ctx.enter_context(tc.tile_pool(name="results", bufs=IMAGES * CO_TILES // TILES_PER_STORE))
 
         eps = consts.tile([P, 1], F32)
         nc.vector.memset(eps[:], EPS)
@@ -71,44 +72,51 @@ def tile_aattn_pb_kernel(tc, content, mean, std, out_w_words, out_w_scales, out_
             nc.sync.dma_start(out=x[:], in_=content_k[c])
             x_k.append(x)
 
-        def load_modulation(c):
+        def load_std(c):
             s = inputs.tile([P, PACK, PIXELS], BF16, tag="s")
             nc.sync.dma_start(out=s[:], in_=std_k[c])
             std_in.append(s)
+
+        def load_mean(c):
             m = inputs.tile([P, PACK, PIXELS], BF16, tag="m")
             nc.sync.dma_start(out=m[:], in_=mean_k[c])
             mean_in.append(m)
 
-        def load_weight():
+        def load_weight_scales():
             for quadrant in range(4):
                 rows = slice(4 * quadrant, 4 * quadrant + 4)
                 nc.sync.dma_start(
                     out=w_scales[32 * quadrant : 32 * quadrant + 4, :, :].bitcast(I32),
                     in_=out_w_scales[:, rows, :].rearrange("g r n -> r g n").bitcast(I32),
                 )
-            for g in range(PASSES):
-                nc.sync.dma_start(
-                    out=w_words[:, g, :].bitcast(I32),
-                    in_=out_w_words[g].rearrange("p n t -> p (n t)").bitcast(I32),
-                )
+
+        def load_weight_words(g):
+            nc.sync.dma_start(
+                out=w_words[:, g, :].bitcast(I32),
+                in_=out_w_words[g].rearrange("p n t -> p (n t)").bitcast(I32),
+            )
 
         def load_residual(b):
             r = residuals.tile([P, CO_TILES, PIXELS], BF16, tag="r")
             nc.sync.dma_start(out=r[:], in_=content_co[b])
             x_co.append(r)
 
-        for c in range(CHUNKS):
-            if c % PASSES == 0:
-                for g in range(PASSES):
-                    load_content(c + g)
-            if c == 0:
+        def on_chunk(stage, c, first=0):
+            if first <= c < CHUNKS:
+                stage(c)
+
+        for s in range(-1, CHUNKS + 2):
+            on_chunk(load_content, s + 1)
+            on_chunk(load_std, s)
+            on_chunk(load_mean, s - 1)
+            if s == 0:
                 nc.sync.dma_start(out=bias_rows[0:CO_TILES, :], in_=out_b.rearrange("(j m) -> j m", m=P))
-            load_modulation(c)
-            if c == PASSES:
-                load_weight()
-            if c > PASSES and c % PASSES == PASSES - 1:
-                load_residual(c // PASSES - 1)
-        load_residual(IMAGES - 1)
+            if s == 1:
+                load_weight_scales()
+            if 0 <= s - 1 < PASSES:
+                load_weight_words(s - 1)
+            if s >= 3 and (s - 3) % PASSES == 0:
+                load_residual((s - 3) // PASSES)
 
         bias = consts.tile([P, CO_TILES], F32)
         with tc.psum_pool(name="setup_psum", bufs=1) as setup_psum:
@@ -151,6 +159,20 @@ def tile_aattn_pb_kernel(tc, content, mean, std, out_w_words, out_w_scales, out_
                 out=sd[c][:], in_=squares[c][:], func=ACT.Sqrt, bias=eps[:], scale=1.0 / (PIXELS - 1)
             )
 
+        def statistics_on_vector(c):
+            moments = stats.tile([P, PACK, 6], F32, tag="moments")
+            mean_var = stats.tile([P, PACK, 2], F32, tag="mean_var")
+            for t in range(PACK):
+                nc.vector.bn_stats(out=moments[:, t, :], in_=x_k[c][:, t, :])
+            for t in range(PACK):
+                nc.vector.bn_aggr(out=mean_var[:, t, :], in_=moments[:, t, :])
+            neg_mu[c] = stats.tile([P, PACK], F32, name="neg_mu", tag="neg_mu")
+            nc.vector.tensor_scalar_mul(out=neg_mu[c][:], in0=mean_var[:, :, 0], scalar1=-1.0)
+            sd[c] = stats.tile([P, PACK], F32, name="sd", tag="sd")
+            nc.scalar.activation(
+                out=sd[c][:], in_=mean_var[:, :, 1], func=ACT.Sqrt, bias=eps[:], scale=PIXELS / (PIXELS - 1.0)
+            )
+
         def centre(c):
             centred[c] = work.tile([P, PACK, PIXELS], F32, name="centred", tag="centred")
             for t in range(PACK):
@@ -181,7 +203,8 @@ def tile_aattn_pb_kernel(tc, content, mean, std, out_w_words, out_w_scales, out_
 
         def regroup(c):
             o_grouped[c] = work.tile([P, PIXELS, PACK], BF16, name="o_grouped", tag="o_grouped", align_bytes=64)
-            nc.scalar.copy(
+            copy = nc.vector.tensor_copy if c < FINISH_LAG - 1 else nc.scalar.copy
+            copy(
                 out=o_grouped[c][:].rearrange("p (n i) t -> p n t i", i=RUN),
                 in_=o_rows[c][:].rearrange("p t (n i) -> p n t i", i=RUN),
             )
@@ -228,21 +251,18 @@ def tile_aattn_pb_kernel(tc, content, mean, std, out_w_words, out_w_scales, out_
                     )
                 nc.sync.dma_start(out=out_co[b, :, first : first + TILES_PER_STORE, :], in_=y[:])
 
-        def on_chunk(stage, c):
-            if 0 <= c < CHUNKS:
-                stage(c)
-
         with tc.manual_schedule():
-            for s in range(-1, CHUNKS + 3):
+            statistics_on_vector(0)
+            for s in range(CHUNKS + FINISH_LAG):
                 on_chunk(centre, s)
                 on_chunk(invert, s - 1)
                 on_chunk(quantise, s - 2)
                 on_chunk(project, s - 2)
                 on_chunk(modulate, s - 1)
-                if 0 <= s - 3 < CHUNKS:
-                    finish((s - 3) // PASSES, (s - 3) % PASSES)
+                if 0 <= s - FINISH_LAG < CHUNKS:
+                    finish((s - FINISH_LAG) // PASSES, (s - FINISH_LAG) % PASSES)
                 on_chunk(sum_pixels, s + 1)
-                on_chunk(sum_squares, s)
+                on_chunk(sum_squares, s, first=1)
                 on_chunk(negate_mean, s + 1)
                 on_chunk(regroup, s - 1)
-                on_chunk(deviation, s)
+                on_chunk(deviation, s, first=1)

@@ -24,7 +24,6 @@ PASSES = CHANNELS // K_PASS
 CHUNKS = IMAGES * PASSES
 CO_TILES = CHANNELS // P
 HALF = CO_TILES // 2
-TILES_PER_STORE = 2
 FINISH_LAG = 3
 RUN = 4
 
@@ -50,7 +49,7 @@ def tile_aattn_pb_kernel(tc, content, mean, std, out_w_words, out_w_scales, out_
         unread = ctx.enter_context(tc.tile_pool(name="unread", bufs=8))
         work = ctx.enter_context(tc.tile_pool(name="work", bufs=3))
         quantised = ctx.enter_context(tc.tile_pool(name="quantised", bufs=2))
-        results = ctx.enter_context(tc.tile_pool(name="results", bufs=IMAGES * CO_TILES // TILES_PER_STORE))
+        results = ctx.enter_context(tc.tile_pool(name="results", bufs=IMAGES * CO_TILES))
 
         eps = consts.tile([P, 1], F32)
         nc.vector.memset(eps[:], EPS)
@@ -64,6 +63,12 @@ def tile_aattn_pb_kernel(tc, content, mean, std, out_w_words, out_w_scales, out_
         nc.vector.memset(w_scales[:].rearrange("p g n -> p (g n)").bitcast(I32), 0)
         identity = consts.tile([P, P], BF16)
         make_identity(nc, identity[:])
+        for quadrant in range(4):
+            rows = slice(4 * quadrant, 4 * quadrant + 4)
+            nc.gpsimd.dma_start(
+                out=w_scales[32 * quadrant : 32 * quadrant + 4, :, :].bitcast(F32),
+                in_=out_w_scales[:, rows, :].rearrange("g r n -> r g n").bitcast(F32),
+            )
 
         x_k, std_in, mean_in, x_co = [], [], [], []
 
@@ -81,14 +86,6 @@ def tile_aattn_pb_kernel(tc, content, mean, std, out_w_words, out_w_scales, out_
             m = inputs.tile([P, PACK, PIXELS], BF16, tag="m")
             nc.sync.dma_start(out=m[:], in_=mean_k[c])
             mean_in.append(m)
-
-        def load_weight_scales():
-            for quadrant in range(4):
-                rows = slice(4 * quadrant, 4 * quadrant + 4)
-                nc.sync.dma_start(
-                    out=w_scales[32 * quadrant : 32 * quadrant + 4, :, :].bitcast(I32),
-                    in_=out_w_scales[:, rows, :].rearrange("g r n -> r g n").bitcast(I32),
-                )
 
         def load_weight_words(g):
             nc.sync.dma_start(
@@ -108,15 +105,13 @@ def tile_aattn_pb_kernel(tc, content, mean, std, out_w_words, out_w_scales, out_
         for s in range(-1, CHUNKS + 2):
             on_chunk(load_content, s + 1)
             on_chunk(load_std, s)
+            if 0 <= s - 2 < PASSES:
+                load_weight_words(s - 2)
             on_chunk(load_mean, s - 1)
             if s == 0:
                 nc.sync.dma_start(out=bias_rows[0:CO_TILES, :], in_=out_b.rearrange("(j m) -> j m", m=P))
-            if s == 1:
-                load_weight_scales()
-            if 0 <= s - 1 < PASSES:
-                load_weight_words(s - 1)
-            if s >= 3 and (s - 3) % PASSES == 0:
-                load_residual((s - 3) // PASSES)
+            if s >= FINISH_LAG and (s - FINISH_LAG) % PASSES == 0:
+                load_residual((s - FINISH_LAG) // PASSES)
 
         bias = consts.tile([P, CO_TILES], F32)
         with tc.psum_pool(name="setup_psum", bufs=1) as setup_psum:
@@ -237,19 +232,17 @@ def tile_aattn_pb_kernel(tc, content, mean, std, out_w_words, out_w_scales, out_
                 )
 
         def finish(b, half):
-            for first in range(half * HALF, (half + 1) * HALF, TILES_PER_STORE):
-                y = results.tile([P, TILES_PER_STORE, PIXELS], F32, tag="y")
-                for i in range(TILES_PER_STORE):
-                    j = first + i
-                    nc.vector.scalar_tensor_tensor(
-                        out=y[:, i, :],
-                        in0=acc[b, j][:],
-                        scalar=bias[:, j : j + 1],
-                        in1=x_co[b][:, j, :],
-                        op0=ALU.add,
-                        op1=ALU.add,
-                    )
-                nc.sync.dma_start(out=out_co[b, :, first : first + TILES_PER_STORE, :], in_=y[:])
+            for j in range(half * HALF, (half + 1) * HALF):
+                y = results.tile([P, PIXELS], F32, tag="y")
+                nc.vector.scalar_tensor_tensor(
+                    out=y[:],
+                    in0=acc[b, j][:],
+                    scalar=bias[:, j : j + 1],
+                    in1=x_co[b][:, j, :],
+                    op0=ALU.add,
+                    op1=ALU.add,
+                )
+                nc.sync.dma_start(out=out_co[b, :, j, :], in_=y[:])
 
         with tc.manual_schedule():
             statistics_on_vector(0)

@@ -63,18 +63,15 @@ def tile_aattn_pb_kernel(tc, content, mean, std, out_w_words, out_w_scales, out_
         nc.vector.memset(w_scales[:].rearrange("p g n -> p (g n)").bitcast(I32), 0)
         identity = consts.tile([P, P], BF16)
         make_identity(nc, identity[:])
-        for quadrant in range(4):
-            rows = slice(4 * quadrant, 4 * quadrant + 4)
-            nc.gpsimd.dma_start(
-                out=w_scales[32 * quadrant : 32 * quadrant + 4, :, :].bitcast(F32),
-                in_=out_w_scales[:, rows, :].rearrange("g r n -> r g n").bitcast(F32),
-            )
-
         x_k, std_in, mean_in, x_co = [], [], [], []
 
         def load_content(c):
             x = inputs.tile([P, PACK, PIXELS], BF16, tag="x")
-            nc.sync.dma_start(out=x[:], in_=content_k[c])
+            if c == 0:
+                for t in range(PACK):
+                    nc.sync.dma_start(out=x[:, t, :], in_=content_k[c][:, t, :])
+            else:
+                nc.sync.dma_start(out=x[:], in_=content_k[c])
             x_k.append(x)
 
         def load_std(c):
@@ -110,6 +107,12 @@ def tile_aattn_pb_kernel(tc, content, mean, std, out_w_words, out_w_scales, out_
             on_chunk(load_mean, s - 1)
             if s == 0:
                 nc.sync.dma_start(out=bias_rows[0:CO_TILES, :], in_=out_b.rearrange("(j m) -> j m", m=P))
+                for quadrant in range(4):
+                    rows = slice(4 * quadrant, 4 * quadrant + 4)
+                    nc.sync.dma_start(
+                        out=w_scales[32 * quadrant : 32 * quadrant + 4, :, :].bitcast(I32),
+                        in_=out_w_scales[:, rows, :].rearrange("g r n -> r g n").bitcast(I32),
+                    )
             if s >= FINISH_LAG and (s - FINISH_LAG) % PASSES == 0:
                 load_residual((s - FINISH_LAG) // PASSES)
 
@@ -125,16 +128,16 @@ def tile_aattn_pb_kernel(tc, content, mean, std, out_w_words, out_w_scales, out_
         centred, o_rows, o_grouped, o_words, o_scales, acc = {}, {}, {}, {}, {}, {}
 
         def sum_pixels(c):
-            total[c] = stats.tile([P, PACK], F32, name="total", tag="total")
+            neg_mu[c] = stats.tile([P, PACK], F32, name="neg_mu", tag="neg_mu")
             for t in range(PACK):
                 copy_out = unread.tile([P, PIXELS], BF16, tag="unread")
                 nc.scalar.activation(
-                    out=copy_out[:], in_=x_k[c][:, t, :], func=ACT.Identity, accum_out=total[c][:, t : t + 1]
+                    out=copy_out[:],
+                    in_=x_k[c][:, t, :],
+                    func=ACT.Identity,
+                    scale=-1.0 / PIXELS,
+                    accum_out=neg_mu[c][:, t : t + 1],
                 )
-
-        def negate_mean(c):
-            neg_mu[c] = stats.tile([P, PACK], F32, name="neg_mu", tag="neg_mu")
-            nc.scalar.mul(out=neg_mu[c][:], in_=total[c][:], mul=-1.0 / PIXELS)
 
         def sum_squares(c):
             squares[c] = stats.tile([P, PACK], F32, name="squares", tag="squares")
@@ -198,7 +201,7 @@ def tile_aattn_pb_kernel(tc, content, mean, std, out_w_words, out_w_scales, out_
 
         def regroup(c):
             o_grouped[c] = work.tile([P, PIXELS, PACK], BF16, name="o_grouped", tag="o_grouped", align_bytes=64)
-            copy = nc.vector.tensor_copy if c < FINISH_LAG - 1 else nc.scalar.copy
+            copy = nc.vector.tensor_copy if c < 1 else nc.scalar.copy
             copy(
                 out=o_grouped[c][:].rearrange("p (n i) t -> p n t i", i=RUN),
                 in_=o_rows[c][:].rearrange("p t (n i) -> p n t i", i=RUN),
@@ -245,6 +248,7 @@ def tile_aattn_pb_kernel(tc, content, mean, std, out_w_words, out_w_scales, out_
                 nc.sync.dma_start(out=out_co[b, :, j, :], in_=y[:])
 
         with tc.manual_schedule():
+            sum_pixels(1)
             statistics_on_vector(0)
             for s in range(CHUNKS + FINISH_LAG):
                 on_chunk(centre, s)
@@ -254,8 +258,7 @@ def tile_aattn_pb_kernel(tc, content, mean, std, out_w_words, out_w_scales, out_
                 on_chunk(modulate, s - 1)
                 if 0 <= s - FINISH_LAG < CHUNKS:
                     finish((s - FINISH_LAG) // PASSES, (s - FINISH_LAG) % PASSES)
-                on_chunk(sum_pixels, s + 1)
+                on_chunk(sum_pixels, s + 1, first=2)
                 on_chunk(sum_squares, s, first=1)
-                on_chunk(negate_mean, s + 1)
                 on_chunk(regroup, s - 1)
                 on_chunk(deviation, s, first=1)

@@ -54,7 +54,7 @@ def tile_aattn_pb_kernel(tc, content, mean, std, out_w_words, out_w_scales, out_
         eps = consts.tile([P, 1], F32)
         nc.vector.memset(eps[:], EPS)
         table_warm = consts.tile([P, 1], F32)
-        nc.scalar.activation(out=table_warm[:], in_=eps[:], func=ACT.Sqrt)
+        nc.scalar.activation(out=table_warm[:], in_=eps[:], func=ACT.Abs_reciprocal_sqrt)
 
         bias_rows = consts.tile([P, P], BF16)
         nc.vector.memset(bias_rows[:].bitcast(I32), 0)
@@ -152,9 +152,13 @@ def tile_aattn_pb_kernel(tc, content, mean, std, out_w_words, out_w_scales, out_
                 )
 
         def deviation(c):
-            sd[c] = stats.tile([P, PACK], F32, name="sd", tag="sd")
+            rstd[c] = stats.tile([P, PACK], F32, name="rstd", tag="rstd")
             nc.scalar.activation(
-                out=sd[c][:], in_=squares[c][:], func=ACT.Sqrt, bias=eps[:], scale=1.0 / (PIXELS - 1)
+                out=rstd[c][:],
+                in_=squares[c][:],
+                func=ACT.Abs_reciprocal_sqrt,
+                bias=eps[:],
+                scale=1.0 / (PIXELS - 1),
             )
 
         def statistics_on_vector(c):
@@ -166,9 +170,13 @@ def tile_aattn_pb_kernel(tc, content, mean, std, out_w_words, out_w_scales, out_
                 nc.vector.bn_aggr(out=mean_var[:, t, :], in_=moments[:, t, :])
             neg_mu[c] = stats.tile([P, PACK], F32, name="neg_mu", tag="neg_mu")
             nc.vector.tensor_scalar_mul(out=neg_mu[c][:], in0=mean_var[:, :, 0], scalar1=-1.0)
-            sd[c] = stats.tile([P, PACK], F32, name="sd", tag="sd")
+            rstd[c] = stats.tile([P, PACK], F32, name="rstd", tag="rstd")
             nc.scalar.activation(
-                out=sd[c][:], in_=mean_var[:, :, 1], func=ACT.Sqrt, bias=eps[:], scale=PIXELS / (PIXELS - 1.0)
+                out=rstd[c][:],
+                in_=mean_var[:, :, 1],
+                func=ACT.Abs_reciprocal_sqrt,
+                bias=eps[:],
+                scale=PIXELS / (PIXELS - 1.0),
             )
 
         def centre(c):
@@ -182,10 +190,6 @@ def tile_aattn_pb_kernel(tc, content, mean, std, out_w_words, out_w_scales, out_
                     op0=ALU.add,
                     op1=ALU.mult,
                 )
-
-        def invert(c):
-            rstd[c] = stats.tile([P, PACK], F32, name="rstd", tag="rstd")
-            nc.vector.reciprocal(out=rstd[c][:], in_=sd[c][:])
 
         def modulate(c):
             o_rows[c] = work.tile([P, PACK, PIXELS], BF16, name="o_rows", tag="o_rows")
@@ -252,7 +256,6 @@ def tile_aattn_pb_kernel(tc, content, mean, std, out_w_words, out_w_scales, out_
             statistics_on_vector(0)
             for s in range(CHUNKS + FINISH_LAG):
                 on_chunk(centre, s)
-                on_chunk(invert, s - 1)
                 on_chunk(quantise, s - 2)
                 on_chunk(project, s - 2)
                 on_chunk(modulate, s - 1)
@@ -260,5 +263,5 @@ def tile_aattn_pb_kernel(tc, content, mean, std, out_w_words, out_w_scales, out_
                     finish((s - FINISH_LAG) // PASSES, (s - FINISH_LAG) % PASSES)
                 on_chunk(sum_pixels, s + 1, first=2)
                 on_chunk(sum_squares, s, first=1)
-                on_chunk(regroup, s - 1)
                 on_chunk(deviation, s, first=1)
+                on_chunk(regroup, s - 1)

@@ -205,7 +205,7 @@ def tile_aattn_pb_kernel(tc, content, mean, std, out_w_words, out_w_scales, out_
 
         def regroup(c):
             o_grouped[c] = work.tile([P, PIXELS, PACK], BF16, name="o_grouped", tag="o_grouped", align_bytes=64)
-            copy = nc.vector.tensor_copy if c < 1 else nc.scalar.copy
+            copy = nc.vector.tensor_copy if c < 2 else nc.scalar.copy
             copy(
                 out=o_grouped[c][:].rearrange("p (n i) t -> p n t i", i=RUN),
                 in_=o_rows[c][:].rearrange("p t (n i) -> p n t i", i=RUN),

@@ -63,6 +63,12 @@ def tile_aattn_pb_kernel(tc, content, mean, std, out_w_words, out_w_scales, out_
         nc.vector.memset(w_scales[:].rearrange("p g n -> p (g n)").bitcast(I32), 0)
         identity = consts.tile([P, P], BF16)
         make_identity(nc, identity[:])
+        for quadrant in range(4):
+            rows = slice(4 * quadrant, 4 * quadrant + 4)
+            nc.gpsimd.dma_start(
+                out=w_scales[32 * quadrant : 32 * quadrant + 4, :, :].bitcast(F32),
+                in_=out_w_scales[:, rows, :].rearrange("g r n -> r g n").bitcast(F32),
+            )
         x_k, std_in, mean_in, x_co = [], [], [], []
 
         def load_content(c):
@@ -107,12 +113,6 @@ def tile_aattn_pb_kernel(tc, content, mean, std, out_w_words, out_w_scales, out_
             on_chunk(load_mean, s - 1)
             if s == 0:
                 nc.sync.dma_start(out=bias_rows[0:CO_TILES, :], in_=out_b.rearrange("(j m) -> j m", m=P))
-                for quadrant in range(4):
-                    rows = slice(4 * quadrant, 4 * quadrant + 4)
-                    nc.sync.dma_start(
-                        out=w_scales[32 * quadrant : 32 * quadrant + 4, :, :].bitcast(I32),
-                        in_=out_w_scales[:, rows, :].rearrange("g r n -> r g n").bitcast(I32),
-                    )
             if s >= FINISH_LAG and (s - FINISH_LAG) % PASSES == 0:
                 load_residual((s - FINISH_LAG) // PASSES)
 

@@ -96,16 +96,18 @@ def tile_aattn_pb_kernel(tc, content, mean, std, out_w_words, out_w_scales, out_
                 in_=out_w_words[g].rearrange("p n t -> p (n t)").bitcast(I32),
             )
 
-        def load_residual(b):
-            r = residuals.tile([P, CO_TILES, PIXELS], BF16, tag="r")
-            nc.sync.dma_start(out=r[:], in_=content_co[b])
-            x_co.append(r)
+        def load_residual(b, half):
+            if half == 0:
+                r = residuals.tile([P, CO_TILES, PIXELS], BF16, tag="r")
+                x_co.append(r)
+            tiles = slice(half * HALF, (half + 1) * HALF)
+            nc.sync.dma_start(out=x_co[b][:, tiles, :], in_=content_co[b][:, tiles, :])
 
         def on_chunk(stage, c, first=0):
             if first <= c < CHUNKS:
                 stage(c)
 
-        for s in range(-1, CHUNKS + 2):
+        for s in range(-1, CHUNKS + FINISH_LAG):
             on_chunk(load_content, s + 1)
             on_chunk(load_std, s)
             if 0 <= s - 2 < PASSES:
@@ -113,8 +115,8 @@ def tile_aattn_pb_kernel(tc, content, mean, std, out_w_words, out_w_scales, out_
             on_chunk(load_mean, s - 1)
             if s == 0:
                 nc.sync.dma_start(out=bias_rows[0:CO_TILES, :], in_=out_b.rearrange("(j m) -> j m", m=P))
-            if s >= FINISH_LAG and (s - FINISH_LAG) % PASSES == 0:
-                load_residual((s - FINISH_LAG) // PASSES)
+            if s >= FINISH_LAG:
+                load_residual((s - FINISH_LAG) // 2, (s - FINISH_LAG) % 2)
 
         bias = consts.tile([P, CO_TILES], F32)
         with tc.psum_pool(name="setup_psum", bufs=1) as setup_psum:

@@ -24,6 +24,9 @@ PASSES = CHANNELS // K_PASS
 CHUNKS = IMAGES * PASSES
 CO_TILES = CHANNELS // P
 HALF = CO_TILES // 2
+EARLY = 6
+FOLD = 32
+FOLDED = range(2, CHUNKS)
 FINISH_LAG = 3
 RUN = 4
 
@@ -63,6 +66,8 @@ def tile_aattn_pb_kernel(tc, content, mean, std, out_w_words, out_w_scales, out_
         nc.vector.memset(w_scales[:].rearrange("p g n -> p (g n)").bitcast(I32), 0)
         identity = consts.tile([P, P], BF16)
         make_identity(nc, identity[:])
+        minus_mean = consts.tile([P, P], BF16)
+        nc.vector.tensor_scalar_mul(out=minus_mean[:], in0=identity[:], scalar1=-1.0 / PIXELS)
         for quadrant in range(4):
             rows = slice(4 * quadrant, 4 * quadrant + 4)
             nc.gpsimd.dma_start(
@@ -124,10 +129,29 @@ def tile_aattn_pb_kernel(tc, content, mean, std, out_w_words, out_w_scales, out_
             nc.tensor.transpose(out=bias_cols[:], in_=bias_rows[:], identity=identity[:])
             nc.vector.tensor_copy(out=bias[:], in_=bias_cols[:, 0:CO_TILES])
 
-        banks = ctx.enter_context(tc.psum_pool(name="banks", bufs=CO_TILES))
+        banks = ctx.enter_context(tc.psum_pool(name="banks", bufs=EARLY))
+        late_bank = ctx.enter_context(tc.psum_pool(name="late_bank", bufs=1))
+        fold_bank = ctx.enter_context(tc.psum_pool(name="fold_bank", bufs=1))
 
         total, neg_mu, squares, sd, rstd = {}, {}, {}, {}, {}
         centred, o_rows, o_grouped, o_words, o_scales, acc = {}, {}, {}, {}, {}, {}
+        folded = {}
+
+        def fold_pixels(c):
+            folded[c] = fold_bank.tile([P, PACK, FOLD], F32, name="folded", tag="fold")
+            pieces = PIXELS // FOLD
+            for i in range(pieces):
+                nc.tensor.matmul(
+                    out=folded[c][:],
+                    lhsT=minus_mean[:],
+                    rhs=x_k[c][:, :, i * FOLD : (i + 1) * FOLD],
+                    start=(i == 0),
+                    stop=(i == pieces - 1),
+                )
+
+        def sum_folded(c):
+            neg_mu[c] = stats.tile([P, PACK], F32, name="neg_mu", tag="neg_mu")
+            nc.vector.tensor_reduce(out=neg_mu[c][:], in_=folded[c][:], axis=mybir.AxisListType.X, op=ALU.add)
 
         def sum_pixels(c):
             neg_mu[c] = stats.tile([P, PACK], F32, name="neg_mu", tag="neg_mu")
@@ -207,8 +231,7 @@ def tile_aattn_pb_kernel(tc, content, mean, std, out_w_words, out_w_scales, out_
 
         def regroup(c):
             o_grouped[c] = work.tile([P, PIXELS, PACK], BF16, name="o_grouped", tag="o_grouped", align_bytes=64)
-            copy = nc.vector.tensor_copy if c < 2 else nc.scalar.copy
-            copy(
+            nc.scalar.copy(
                 out=o_grouped[c][:].rearrange("p (n i) t -> p n t i", i=RUN),
                 in_=o_rows[c][:].rearrange("p t (n i) -> p n t i", i=RUN),
             )
@@ -224,28 +247,45 @@ def tile_aattn_pb_kernel(tc, content, mean, std, out_w_words, out_w_scales, out_
                 in_=o_grouped[c][:].rearrange("p n t -> p (n t)"),
             )
 
+        def multiply(b, g, j, bank):
+            cols = slice(j * P, (j + 1) * P)
+            nc.tensor.matmul_mx(
+                out=bank,
+                lhsT=w_words[:, g, cols].bitcast(FP8X4),
+                lhsT_scale=w_scales[:, g, cols],
+                rhs=o_words[b][:, g, :].bitcast(FP8X4),
+                rhs_scale=o_scales[b][:, g, :],
+                start=(g == 0),
+                stop=(g == PASSES - 1),
+            )
+
         def project(c):
             b, g = divmod(c, PASSES)
-            for j in range(CO_TILES):
+            last = b == IMAGES - 1
+            early = CO_TILES if last else EARLY
+            for j in range(early):
                 if g == 0:
-                    acc[b, j] = banks.tile([P, PIXELS], F32, name="bank", tag="bank")
-                cols = slice(j * P, (j + 1) * P)
-                nc.tensor.matmul_mx(
-                    out=acc[b, j][:],
-                    lhsT=w_words[:, g, cols].bitcast(FP8X4),
-                    lhsT_scale=w_scales[:, g, cols],
-                    rhs=o_words[b][:, g, :].bitcast(FP8X4),
-                    rhs_scale=o_scales[b][:, g, :],
-                    start=(g == 0),
-                    stop=(g == PASSES - 1),
-                )
+                    if j < EARLY:
+                        bank = banks.tile([P, PIXELS], F32, name="bank", tag="bank")
+                    elif j == EARLY:
+                        bank = late_bank.tile([P, PIXELS], F32, name="late_one", tag="late")
+                    else:
+                        bank = fold_bank.tile([P, PIXELS], F32, name="fold_one", tag="fold")
+                    acc[b, j] = bank[:]
+                multiply(b, g, j, acc[b, j])
+            if g == PASSES - 1 and not last:
+                pair = late_bank.tile([P, CO_TILES - EARLY, PIXELS], F32, name="pair", tag="late")
+                for j in range(EARLY, CO_TILES):
+                    acc[b, j] = pair[:, j - EARLY, :]
+                    for both in range(PASSES):
+                        multiply(b, both, j, acc[b, j])
 
         def finish(b, half):
             for j in range(half * HALF, (half + 1) * HALF):
                 y = results.tile([P, PIXELS], F32, tag="y")
                 nc.vector.scalar_tensor_tensor(
                     out=y[:],
-                    in0=acc[b, j][:],
+                    in0=acc[b, j],
                     scalar=bias[:, j : j + 1],
                     in1=x_co[b][:, j, :],
                     op0=ALU.add,
@@ -257,13 +297,14 @@ def tile_aattn_pb_kernel(tc, content, mean, std, out_w_words, out_w_scales, out_
             sum_pixels(1)
             statistics_on_vector(0)
             for s in range(CHUNKS + FINISH_LAG):
+                on_chunk(fold_pixels, s + 1, first=FOLDED.start)
                 on_chunk(centre, s)
                 on_chunk(quantise, s - 2)
                 on_chunk(project, s - 2)
                 on_chunk(modulate, s - 1)
+                on_chunk(sum_folded, s + 1, first=FOLDED.start)
                 if 0 <= s - FINISH_LAG < CHUNKS:
                     finish((s - FINISH_LAG) // PASSES, (s - FINISH_LAG) % PASSES)
-                on_chunk(sum_pixels, s + 1, first=2)
                 on_chunk(sum_squares, s, first=1)
                 on_chunk(deviation, s, first=1)
                 on_chunk(regroup, s - 1)

@@ -27,6 +27,7 @@ HALF = CO_TILES // 2
 EARLY = 6
 FOLD = 32
 FOLDED = range(2, CHUNKS)
+SHARED = range(2, 6)
 FINISH_LAG = 3
 RUN = 4
 
@@ -165,9 +166,10 @@ def tile_aattn_pb_kernel(tc, content, mean, std, out_w_words, out_w_scales, out_
                     accum_out=neg_mu[c][:, t : t + 1],
                 )
 
-        def sum_squares(c):
-            squares[c] = stats.tile([P, PACK], F32, name="squares", tag="squares")
-            for t in range(PACK):
+        def sum_squares(c, slabs):
+            if slabs.start == 0:
+                squares[c] = stats.tile([P, PACK], F32, name="squares", tag="squares")
+            for t in slabs:
                 square_out = unread.tile([P, PIXELS], BF16, tag="unread")
                 nc.scalar.activation(
                     out=square_out[:],
@@ -219,7 +221,7 @@ def tile_aattn_pb_kernel(tc, content, mean, std, out_w_words, out_w_scales, out_
 
         def modulate(c):
             o_rows[c] = work.tile([P, PACK, PIXELS], BF16, name="o_rows", tag="o_rows")
-            for t in range(PACK):
+            for t in range(PACK - 1 if c in SHARED else PACK):
                 nc.vector.scalar_tensor_tensor(
                     out=o_rows[c][:, t, :],
                     in0=centred[c][:, t, :],
@@ -228,6 +230,16 @@ def tile_aattn_pb_kernel(tc, content, mean, std, out_w_words, out_w_scales, out_
                     op0=ALU.mult,
                     op1=ALU.add,
                 )
+
+        def modulate_last_slab(c):
+            if c not in SHARED:
+                return
+            t = PACK - 1
+            scaled = centred[c][:, 1, :]
+            nc.scalar.activation(
+                out=scaled, in_=centred[c][:, t, :], func=ACT.Copy, scale=rstd[c][:, t : t + 1]
+            )
+            nc.gpsimd.tensor_tensor(out=o_rows[c][:, t, :], in0=scaled, in1=mean_in[c][:, t, :], op=ALU.add)
 
         def regroup(c):
             o_grouped[c] = work.tile([P, PIXELS, PACK], BF16, name="o_grouped", tag="o_grouped", align_bytes=64)
@@ -305,6 +317,8 @@ def tile_aattn_pb_kernel(tc, content, mean, std, out_w_words, out_w_scales, out_
                 on_chunk(sum_folded, s + 1, first=FOLDED.start)
                 if 0 <= s - FINISH_LAG < CHUNKS:
                     finish((s - FINISH_LAG) // PASSES, (s - FINISH_LAG) % PASSES)
-                on_chunk(sum_squares, s, first=1)
+                on_chunk(lambda c: sum_squares(c, range(0, PACK - 1)), s, first=1)
+                on_chunk(modulate_last_slab, s - 1)
+                on_chunk(lambda c: sum_squares(c, range(PACK - 1, PACK)), s, first=1)
                 on_chunk(deviation, s, first=1)
                 on_chunk(regroup, s - 1)

@@ -27,8 +27,8 @@ HALF = CO_TILES // 2
 EARLY = 6
 FOLD = 32
 FOLDED = range(2, CHUNKS)
-SHARED = range(2, 6)
-FINISH_LAG = 3
+SHARED = range(3, CHUNKS - 2)
+FINISH_LAG = 4
 RUN = 4
 
 FLOPS = 2 * IMAGES * PIXELS * CHANNELS * CHANNELS
@@ -166,10 +166,9 @@ def tile_aattn_pb_kernel(tc, content, mean, std, out_w_words, out_w_scales, out_
                     accum_out=neg_mu[c][:, t : t + 1],
                 )
 
-        def sum_squares(c, slabs):
-            if slabs.start == 0:
-                squares[c] = stats.tile([P, PACK], F32, name="squares", tag="squares")
-            for t in slabs:
+        def sum_squares(c):
+            squares[c] = stats.tile([P, PACK], F32, name="squares", tag="squares")
+            for t in range(PACK):
                 square_out = unread.tile([P, PIXELS], BF16, tag="unread")
                 nc.scalar.activation(
                     out=square_out[:],
@@ -309,16 +308,15 @@ def tile_aattn_pb_kernel(tc, content, mean, std, out_w_words, out_w_scales, out_
             sum_pixels(1)
             statistics_on_vector(0)
             for s in range(CHUNKS + FINISH_LAG):
-                on_chunk(fold_pixels, s + 1, first=FOLDED.start)
                 on_chunk(centre, s)
-                on_chunk(quantise, s - 2)
-                on_chunk(project, s - 2)
                 on_chunk(modulate, s - 1)
                 on_chunk(sum_folded, s + 1, first=FOLDED.start)
                 if 0 <= s - FINISH_LAG < CHUNKS:
                     finish((s - FINISH_LAG) // PASSES, (s - FINISH_LAG) % PASSES)
-                on_chunk(lambda c: sum_squares(c, range(0, PACK - 1)), s, first=1)
+                on_chunk(fold_pixels, s + 2, first=FOLDED.start)
+                on_chunk(quantise, s - 2)
+                on_chunk(project, s - 2)
                 on_chunk(modulate_last_slab, s - 1)
-                on_chunk(lambda c: sum_squares(c, range(PACK - 1, PACK)), s, first=1)
+                on_chunk(sum_squares, s, first=1)
                 on_chunk(deviation, s, first=1)
                 on_chunk(regroup, s - 1)

@@ -25,7 +25,7 @@ CHUNKS = IMAGES * PASSES
 CO_TILES = CHANNELS // P
 HALF = CO_TILES // 2
 EARLY = 6
-FOLD = 32
+FOLD = 16
 FOLDED = range(2, CHUNKS)
 SHARED = range(3, CHUNKS - 2)
 FINISH_LAG = 4

from contextlib import ExitStack

import concourse.mybir as mybir
from concourse.masks import make_identity

F32 = mybir.dt.float32
BF16 = mybir.dt.bfloat16
I32 = mybir.dt.int32
U32 = mybir.dt.uint32
U8 = mybir.dt.uint8
FP8X4 = mybir.dt.float8_e4m3fn_x4
ACT = mybir.ActivationFunctionType
ALU = mybir.AluOpType

IMAGES = 4
CHANNELS = 1024
PIXELS = 256
EPS = 1e-5

P = 128
PACK = 4
K_PASS = P * PACK
PASSES = CHANNELS // K_PASS
CHUNKS = IMAGES * PASSES
CO_TILES = CHANNELS // P
HALF = CO_TILES // 2
EARLY = 6
FOLD = 16
FOLDED = range(2, CHUNKS)
SHARED = range(3, CHUNKS - 2)
FINISH_LAG = 4
RUN = 4

FLOPS = 2 * IMAGES * PIXELS * CHANNELS * CHANNELS


def tile_aattn_pb_kernel(tc, content, mean, std, out_w_words, out_w_scales, out_b, out):
    nc = tc.nc

    by_k = "b (g p t) h w -> (b g) p t (h w)"
    by_co = "b (j m) h w -> b m j (h w)"
    content_k = content.rearrange(by_k, g=PASSES, p=P, t=PACK)
    std_k = std.rearrange(by_k, g=PASSES, p=P, t=PACK)
    mean_k = mean.rearrange(by_k, g=PASSES, p=P, t=PACK)
    content_co = content.rearrange(by_co, m=P)
    out_co = out.rearrange(by_co, m=P)

    with ExitStack() as ctx:
        consts = ctx.enter_context(tc.tile_pool(name="consts", bufs=1))
        inputs = ctx.enter_context(tc.tile_pool(name="inputs", bufs=CHUNKS))
        residuals = ctx.enter_context(tc.tile_pool(name="residuals", bufs=IMAGES))
        stats = ctx.enter_context(tc.tile_pool(name="stats", bufs=4))
        unread = ctx.enter_context(tc.tile_pool(name="unread", bufs=8))
        work = ctx.enter_context(tc.tile_pool(name="work", bufs=3))
        quantised = ctx.enter_context(tc.tile_pool(name="quantised", bufs=2))
        results = ctx.enter_context(tc.tile_pool(name="results", bufs=IMAGES * CO_TILES))

        eps = consts.tile([P, 1], F32)
        nc.vector.memset(eps[:], EPS)
        table_warm = consts.tile([P, 1], F32)
        nc.scalar.activation(out=table_warm[:], in_=eps[:], func=ACT.Abs_reciprocal_sqrt)

        bias_rows = consts.tile([P, P], BF16)
        nc.vector.memset(bias_rows[:].bitcast(I32), 0)
        w_words = consts.tile([P, PASSES, CHANNELS], U32, align_bytes=64)
        w_scales = consts.tile([P, PASSES, CHANNELS], U8, align_bytes=64)
        nc.vector.memset(w_scales[:].rearrange("p g n -> p (g n)").bitcast(I32), 0)
        identity = consts.tile([P, P], BF16)
        make_identity(nc, identity[:])
        minus_mean = consts.tile([P, P], BF16)
        nc.vector.tensor_scalar_mul(out=minus_mean[:], in0=identity[:], scalar1=-1.0 / PIXELS)
        for quadrant in range(4):
            rows = slice(4 * quadrant, 4 * quadrant + 4)
            nc.gpsimd.dma_start(
                out=w_scales[32 * quadrant : 32 * quadrant + 4, :, :].bitcast(F32),
                in_=out_w_scales[:, rows, :].rearrange("g r n -> r g n").bitcast(F32),
            )
        x_k, std_in, mean_in, x_co = [], [], [], []

        def load_content(c):
            x = inputs.tile([P, PACK, PIXELS], BF16, tag="x")
            if c == 0:
                for t in range(PACK):
                    nc.sync.dma_start(out=x[:, t, :], in_=content_k[c][:, t, :])
            else:
                nc.sync.dma_start(out=x[:], in_=content_k[c])
            x_k.append(x)

        def load_std(c):
            s = inputs.tile([P, PACK, PIXELS], BF16, tag="s")
            nc.sync.dma_start(out=s[:], in_=std_k[c])
            std_in.append(s)

        def load_mean(c):
            m = inputs.tile([P, PACK, PIXELS], BF16, tag="m")
            nc.sync.dma_start(out=m[:], in_=mean_k[c])
            mean_in.append(m)

        def load_weight_words(g):
            nc.sync.dma_start(
                out=w_words[:, g, :].bitcast(I32),
                in_=out_w_words[g].rearrange("p n t -> p (n t)").bitcast(I32),
            )

        def load_residual(b, half):
            if half == 0:
                r = residuals.tile([P, CO_TILES, PIXELS], BF16, tag="r")
                x_co.append(r)
            tiles = slice(half * HALF, (half + 1) * HALF)
            nc.sync.dma_start(out=x_co[b][:, tiles, :], in_=content_co[b][:, tiles, :])

        def on_chunk(stage, c, first=0):
            if first <= c < CHUNKS:
                stage(c)

        for s in range(-1, CHUNKS + FINISH_LAG):
            on_chunk(load_content, s + 1)
            on_chunk(load_std, s)
            if 0 <= s - 2 < PASSES:
                load_weight_words(s - 2)
            on_chunk(load_mean, s - 1)
            if s == 0:
                nc.sync.dma_start(out=bias_rows[0:CO_TILES, :], in_=out_b.rearrange("(j m) -> j m", m=P))
            if s >= FINISH_LAG:
                load_residual((s - FINISH_LAG) // 2, (s - FINISH_LAG) % 2)

        bias = consts.tile([P, CO_TILES], F32)
        with tc.psum_pool(name="setup_psum", bufs=1) as setup_psum:
            bias_cols = setup_psum.tile([P, P], BF16)
            nc.tensor.transpose(out=bias_cols[:], in_=bias_rows[:], identity=identity[:])
            nc.vector.tensor_copy(out=bias[:], in_=bias_cols[:, 0:CO_TILES])

        banks = ctx.enter_context(tc.psum_pool(name="banks", bufs=EARLY))
        late_bank = ctx.enter_context(tc.psum_pool(name="late_bank", bufs=1))
        fold_bank = ctx.enter_context(tc.psum_pool(name="fold_bank", bufs=1))

        total, neg_mu, squares, sd, rstd = {}, {}, {}, {}, {}
        centred, o_rows, o_grouped, o_words, o_scales, acc = {}, {}, {}, {}, {}, {}
        folded = {}

        def fold_pixels(c):
            folded[c] = fold_bank.tile([P, PACK, FOLD], F32, name="folded", tag="fold")
            pieces = PIXELS // FOLD
            for i in range(pieces):
                nc.tensor.matmul(
                    out=folded[c][:],
                    lhsT=minus_mean[:],
                    rhs=x_k[c][:, :, i * FOLD : (i + 1) * FOLD],
                    start=(i == 0),
                    stop=(i == pieces - 1),
                )

        def sum_folded(c):
            neg_mu[c] = stats.tile([P, PACK], F32, name="neg_mu", tag="neg_mu")
            nc.vector.tensor_reduce(out=neg_mu[c][:], in_=folded[c][:], axis=mybir.AxisListType.X, op=ALU.add)

        def sum_pixels(c):
            neg_mu[c] = stats.tile([P, PACK], F32, name="neg_mu", tag="neg_mu")
            for t in range(PACK):
                copy_out = unread.tile([P, PIXELS], BF16, tag="unread")
                nc.scalar.activation(
                    out=copy_out[:],
                    in_=x_k[c][:, t, :],
                    func=ACT.Identity,
                    scale=-1.0 / PIXELS,
                    accum_out=neg_mu[c][:, t : t + 1],
                )

        def sum_squares(c):
            squares[c] = stats.tile([P, PACK], F32, name="squares", tag="squares")
            for t in range(PACK):
                square_out = unread.tile([P, PIXELS], BF16, tag="unread")
                nc.scalar.activation(
                    out=square_out[:],
                    in_=x_k[c][:, t, :],
                    func=ACT.Square,
                    bias=neg_mu[c][:, t : t + 1],
                    accum_out=squares[c][:, t : t + 1],
                )

        def deviation(c):
            rstd[c] = stats.tile([P, PACK], F32, name="rstd", tag="rstd")
            nc.scalar.activation(
                out=rstd[c][:],
                in_=squares[c][:],
                func=ACT.Abs_reciprocal_sqrt,
                bias=eps[:],
                scale=1.0 / (PIXELS - 1),
            )

        def statistics_on_vector(c):
            moments = stats.tile([P, PACK, 6], F32, tag="moments")
            mean_var = stats.tile([P, PACK, 2], F32, tag="mean_var")
            for t in range(PACK):
                nc.vector.bn_stats(out=moments[:, t, :], in_=x_k[c][:, t, :])
            for t in range(PACK):
                nc.vector.bn_aggr(out=mean_var[:, t, :], in_=moments[:, t, :])
            neg_mu[c] = stats.tile([P, PACK], F32, name="neg_mu", tag="neg_mu")
            nc.vector.tensor_scalar_mul(out=neg_mu[c][:], in0=mean_var[:, :, 0], scalar1=-1.0)
            rstd[c] = stats.tile([P, PACK], F32, name="rstd", tag="rstd")
            nc.scalar.activation(
                out=rstd[c][:],
                in_=mean_var[:, :, 1],
                func=ACT.Abs_reciprocal_sqrt,
                bias=eps[:],
                scale=PIXELS / (PIXELS - 1.0),
            )

        def centre(c):
            centred[c] = work.tile([P, PACK, PIXELS], F32, name="centred", tag="centred")
            for t in range(PACK):
                nc.vector.scalar_tensor_tensor(
                    out=centred[c][:, t, :],
                    in0=x_k[c][:, t, :],
                    scalar=neg_mu[c][:, t : t + 1],
                    in1=std_in[c][:, t, :],
                    op0=ALU.add,
                    op1=ALU.mult,
                )

        def modulate(c):
            o_rows[c] = work.tile([P, PACK, PIXELS], BF16, name="o_rows", tag="o_rows")
            for t in range(PACK - 1 if c in SHARED else PACK):
                nc.vector.scalar_tensor_tensor(
                    out=o_rows[c][:, t, :],
                    in0=centred[c][:, t, :],
                    scalar=rstd[c][:, t : t + 1],
                    in1=mean_in[c][:, t, :],
                    op0=ALU.mult,
                    op1=ALU.add,
                )

        def modulate_last_slab(c):
            if c not in SHARED:
                return
            t = PACK - 1
            scaled = centred[c][:, 1, :]
            nc.scalar.activation(
                out=scaled, in_=centred[c][:, t, :], func=ACT.Copy, scale=rstd[c][:, t : t + 1]
            )
            nc.gpsimd.tensor_tensor(out=o_rows[c][:, t, :], in0=scaled, in1=mean_in[c][:, t, :], op=ALU.add)

        def regroup(c):
            o_grouped[c] = work.tile([P, PIXELS, PACK], BF16, name="o_grouped", tag="o_grouped", align_bytes=64)
            nc.scalar.copy(
                out=o_grouped[c][:].rearrange("p (n i) t -> p n t i", i=RUN),
                in_=o_rows[c][:].rearrange("p t (n i) -> p n t i", i=RUN),
            )

        def quantise(c):
            b, g = divmod(c, PASSES)
            if g == 0:
                o_words[b] = quantised.tile([P, PASSES, PIXELS], U32, name="o_words", tag="o_words", align_bytes=64)
                o_scales[b] = quantised.tile([P, PASSES, PIXELS], U8, name="o_scales", tag="o_scales", align_bytes=64)
            nc.vector.quantize_mx(
                out=o_words[b][:, g, :].bitcast(FP8X4),
                scales=o_scales[b][:, g, :],
                in_=o_grouped[c][:].rearrange("p n t -> p (n t)"),
            )

        def multiply(b, g, j, bank):
            cols = slice(j * P, (j + 1) * P)
            nc.tensor.matmul_mx(
                out=bank,
                lhsT=w_words[:, g, cols].bitcast(FP8X4),
                lhsT_scale=w_scales[:, g, cols],
                rhs=o_words[b][:, g, :].bitcast(FP8X4),
                rhs_scale=o_scales[b][:, g, :],
                start=(g == 0),
                stop=(g == PASSES - 1),
            )

        def project(c):
            b, g = divmod(c, PASSES)
            last = b == IMAGES - 1
            early = CO_TILES if last else EARLY
            for j in range(early):
                if g == 0:
                    if j < EARLY:
                        bank = banks.tile([P, PIXELS], F32, name="bank", tag="bank")
                    elif j == EARLY:
                        bank = late_bank.tile([P, PIXELS], F32, name="late_one", tag="late")
                    else:
                        bank = fold_bank.tile([P, PIXELS], F32, name="fold_one", tag="fold")
                    acc[b, j] = bank[:]
                multiply(b, g, j, acc[b, j])
            if g == PASSES - 1 and not last:
                pair = late_bank.tile([P, CO_TILES - EARLY, PIXELS], F32, name="pair", tag="late")
                for j in range(EARLY, CO_TILES):
                    acc[b, j] = pair[:, j - EARLY, :]
                    for both in range(PASSES):
                        multiply(b, both, j, acc[b, j])

        def finish(b, half):
            for j in range(half * HALF, (half + 1) * HALF):
                y = results.tile([P, PIXELS], F32, tag="y")
                nc.vector.scalar_tensor_tensor(
                    out=y[:],
                    in0=acc[b, j],
                    scalar=bias[:, j : j + 1],
                    in1=x_co[b][:, j, :],
                    op0=ALU.add,
                    op1=ALU.add,
                )
                nc.sync.dma_start(out=out_co[b, :, j, :], in_=y[:])

        with tc.manual_schedule():
            sum_pixels(1)
            statistics_on_vector(0)
            for s in range(CHUNKS + FINISH_LAG):
                on_chunk(centre, s)
                on_chunk(modulate, s - 1)
                on_chunk(sum_folded, s + 1, first=FOLDED.start)
                if 0 <= s - FINISH_LAG < CHUNKS:
                    finish((s - FINISH_LAG) // PASSES, (s - FINISH_LAG) % PASSES)
                on_chunk(fold_pixels, s + 2, first=FOLDED.start)
                on_chunk(quantise, s - 2)
                on_chunk(project, s - 2)
                on_chunk(modulate_last_slab, s - 1)
                on_chunk(sum_squares, s, first=1)
                on_chunk(deviation, s, first=1)
                on_chunk(regroup, s - 1)
